import numpy as np
import ml_dtypes


def mxq(x, axis, fmt="e4m3"):
    dtype, down = {"e4m3": (ml_dtypes.float8_e4m3fn, 7), "e5m2": (ml_dtypes.float8_e5m2, 14)}[fmt]
    v = np.moveaxis(np.asarray(x, np.float32).astype(ml_dtypes.bfloat16).astype(np.float64), axis, -1)
    blocks = v.reshape(v.shape[:-1] + (-1, 32))
    amax = np.abs(blocks).max(-1, keepdims=True)
    byte = np.maximum(np.where(amax > 0, np.frexp(amax)[1] - 1 + 127, 0) - down, 1)
    scale = np.exp2(byte - 127.0)
    codes = (blocks / scale).astype(np.float32).astype(dtype).astype(np.float64)
    return np.moveaxis((codes * scale).reshape(v.shape), -1, axis)


WIDE = False


def mx_kscale(k):
    if not WIDE:
        return np.ones(k)
    levels = np.array([10, -10, 5, -5, 0])
    if k % 512:
        return np.exp2(np.random.permutation(np.resize(levels, k // 32))).repeat(32)
    a = np.empty((k // 512, 16))
    for p in range(k // 512):
        a[p, :8] = np.random.permutation(np.resize(levels, 8))
        for g in range(8):
            far = levels[np.abs(levels - a[p, g]) >= 10]
            a[p, g + 8] = far[np.random.randint(len(far))]
    return np.exp2(a.ravel()).repeat(32)


BF16 = ml_dtypes.bfloat16


def bf(x):
    return np.asarray(x, np.float32).astype(BF16)


def f64(x):
    return np.asarray(x).astype(np.float64)


B, D, H = 4096, 512, 512
M_SCALE = 1.5


def setup_inputs():
    s, t = mx_kscale(D), mx_kscale(H)
    return {'x': bf(np.random.standard_normal((B, D)) * s),
            'h_prev': bf(np.random.standard_normal((B, H)) * t),
            'c_prev': bf(np.random.standard_normal((B, H))),
            'W_ih': bf(np.random.standard_normal((2 * H, D)) * 0.7 / np.sqrt(D) / s[None, :]),
            'b_ih': bf(np.random.standard_normal(2 * H) * 0.2),
            'W_hh': bf(np.random.standard_normal((2 * H, H)) * 0.7 / np.sqrt(H) / t[None, :]),
            'b_hh': bf(np.random.standard_normal(2 * H) * 0.2),
            'log_lambda': bf(np.log(np.random.uniform(0.05, 0.5, H))),
            'z_bias': bf(np.random.standard_normal(H) * 0.2),
            'm_bias': bf(np.random.standard_normal(H) * 0.2)}


def reference(x, h_prev, c_prev, W_ih, b_ih, W_hh, b_hh, log_lambda, z_bias, m_bias):
    gates = ((mxq(f64(x), 1, 'e4m3') @ mxq(f64(W_ih), 1, 'e4m3').T) + f64(b_ih)
             + (mxq(f64(h_prev), 1, 'e4m3') @ mxq(f64(W_hh), 1, 'e4m3').T) + f64(b_hh))
    z_raw, m_raw = gates[:, :H], gates[:, H:]
    z_t = np.tanh(z_raw + f64(z_bias))
    M_t = M_SCALE * np.tanh(m_raw + f64(m_bias))
    A_base = -np.exp(f64(log_lambda))
    innov = z_t - M_t * (A_base * f64(c_prev))
    return z_t, M_t, innov

@@ -1,0 +1,251 @@
+from contextlib import ExitStack
+
+import concourse.mybir as mybir
+from concourse.masks import make_identity
+
+F32 = mybir.dt.float32
+BF16 = mybir.dt.bfloat16
+U32 = mybir.dt.uint32
+U8 = mybir.dt.uint8
+FP8X4 = mybir.dt.float8_e4m3fn_x4
+ACT = mybir.ActivationFunctionType
+ALU = mybir.AluOpType
+
+P = 128
+B, D, H = 4096, 512, 512
+NT = B // P
+TG = 8
+TB = 4
+NB = NT // TB
+M_SCALE = 1.5
+FLOPS = 2 * B * (2 * H) * (D + H)
+
+
+def tile_koslmcell_pa_t_kernel(tc, x, h_prev, c_prev, W_ih, b_ih, W_hh, b_hh,
+                                          log_lambda, z_bias, m_bias, out_0, out_1, out_2):
+    nc = tc.nc
+    with ExitStack() as ctx:
+        const = ctx.enter_context(tc.tile_pool(name="const", bufs=1))
+        resid = ctx.enter_context(tc.tile_pool(name="resid", bufs=1))
+        gpool = ctx.enter_context(tc.tile_pool(name="gpool", bufs=4))
+        qpool = ctx.enter_context(tc.tile_pool(name="qpool", bufs=3))
+        tpool = ctx.enter_context(tc.tile_pool(name="tpool", bufs=8))
+        stage = ctx.enter_context(tc.tile_pool(name="stage", bufs=3))
+        ps = ctx.enter_context(tc.psum_pool(name="ps", bufs=8))
+        ctx.enter_context(tc.manual_schedule())
+
+        def row(v):
+            return v.rearrange("(o n) -> o n", o=1)
+
+        vecs = const.tile([P, 3 * H], BF16, name="vecs")
+        nc.vector.memset(vecs[:], 0.0)
+        ones = const.tile([P, P], BF16, name="ones")
+        nc.vector.memset(ones[:], 1.0)
+        nc.scalar.dma_start(out=vecs[0:1, 0:2 * H], in_=row(b_ih))
+        nc.scalar.dma_start(out=vecs[1:2, 0:2 * H], in_=row(b_hh))
+        nc.scalar.dma_start(out=vecs[2:3, 0:H], in_=row(z_bias))
+        nc.scalar.dma_start(out=vecs[2:3, H:2 * H], in_=row(m_bias))
+        nc.scalar.dma_start(out=vecs[0:1, 2 * H:3 * H], in_=row(log_lambda))
+        ident = const.tile([P, P], F32, name="ident")
+        make_identity(nc, ident[:])
+
+        views = [v.rearrange("(g p t) k -> g p t k", p=P, t=TG) for v in (x, h_prev, c_prev)]
+        outs = [o.rearrange("(g p t) n -> g p t n", p=P, t=TG) for o in (out_0, out_1, out_2)]
+
+        def dram(view, t0, n):
+            return view[t0 // TG, :, t0 % TG:t0 % TG + n, :]
+        where = [{}, {}, {}]
+
+        def load(i, t0, n, tag):
+            rt = resid.tile([P, n * D], BF16, name="in%d_%d" % (i, t0), tag="%s%d" % ("xhc"[i], tag))
+            nc.sync.dma_start(out=rt[:].rearrange("p (t k) -> p t k", k=D), in_=dram(views[i], t0, n))
+            for j in range(n):
+                where[i][t0 + j] = (rt, j)
+
+        def load_w(op, half, tag):
+            w = (W_ih, W_hh)[op]
+            wr = stage.tile([P, 4 * D], BF16, name="wraw%d%d" % (op, half), tag=tag)
+            nc.sync.dma_start(out=wr[:], in_=w[half * H:(half + 1) * H, :].rearrange("(p a) k -> p (a k)", a=4))
+            return wr
+
+        load(0, 0, 4, 0)
+        load(1, 0, 4, 0)
+        wraw = {}
+        wraw[(0, 1)] = load_w(0, 1, "zst")
+        wraw[(1, 1)] = load_w(1, 1, "ist")
+        wraw[(0, 0)] = load_w(0, 0, "zst")
+        wraw[(1, 0)] = load_w(1, 0, "ist")
+        load(0, 4, 4, 4)
+        load(1, 4, 4, 4)
+        load(2, 0, 4, 0)
+        load(0, 8, 8, 8)
+        load(1, 8, 8, 8)
+        load(2, 4, 4, 4)
+        load(0, 16, 8, 16)
+        load(1, 16, 8, 16)
+        load(2, 8, 8, 8)
+        load(2, 16, 8, 16)
+
+        wq = const.tile([P, 2, 2 * H], U32, name="wq", align_bytes=64)
+        wsc = const.tile([P, 2, 2 * H], U8, name="wsc", align_bytes=64)
+
+        def transposes(srcs, label, engines, rows_interleaved=False):
+            grouped = gpool.tile([P, 4 * P, 2], F32, name="grp_" + label, tag="grp", align_bytes=64)
+            for half in range(2):
+                tp = ps.tile([P, 2, 2, P], F32, name="tp_%s_%d" % (label, half), tag="ps")
+                for a in range(2):
+                    for u in range(2):
+                        nc.tensor.transpose(tp[:, a, u, :], srcs[2 * half + a][:, u:2 * P:2], ident[:])
+                if rows_interleaved:
+                    dst = grouped[:].rearrange("p (r a) u -> p r a u", a=4)[:, :, 2 * half:2 * half + 2, :]
+                    src = tp[:].rearrange("p a u r -> p r a u")
+                else:
+                    dst = grouped[:, 2 * P * half:2 * P * (half + 1), :].rearrange("p (a r) u -> p a r u", a=2)
+                    src = tp[:].rearrange("p a u r -> p a r u")
+                if engines[half] == "s":
+                    nc.scalar.copy(out=dst, in_=src)
+                else:
+                    nc.vector.tensor_copy(out=dst, in_=src)
+            return grouped
+
+        def quantise(grouped, codes, scales):
+            nc.vector.quantize_mx(out=codes.bitcast(FP8X4), scales=scales,
+                                  in_=grouped[:].rearrange("p c u -> p (c u)").bitcast(BF16))
+
+        def t1_w(op, half):
+            wv = wraw[(op, half)][:].bitcast(F32)
+            srcs = [wv[:, a * (D // 2):(a + 1) * (D // 2)] for a in range(4)]
+            return transposes(srcs, "w%d%d" % (op, half), ("ss", "vv")[op], rows_interleaved=True)
+
+        def quant_w(g, op, half):
+            quantise(g, wq[:, op, half * H:(half + 1) * H], wsc[:, op, half * H:(half + 1) * H])
+
+        def t1_in(b, op, engines):
+            srcs = []
+            for t in range(b * TB, (b + 1) * TB):
+                rt, j = where[op][t]
+                srcs.append(rt[:].bitcast(F32)[:, j * (D // 2):(j + 1) * (D // 2)])
+            return (transposes(srcs, "b%d_%d" % (b, op), engines), b, op)
+
+        qs = {}
+
+        def quant_in(gbo):
+            g, b, op = gbo
+            q = qpool.tile([P, TB * P], U32, name="q%d_%d" % (b, op), tag="q%d" % op, align_bytes=64)
+            s = qpool.tile([P, TB * P], U8, name="s%d_%d" % (b, op), tag="s%d" % op, align_bytes=64)
+            quantise(g, q[:], s[:])
+            qs[(b, op)] = (q, s)
+
+        tms = {}
+        msts = {}
+
+        def scaled_c(b):
+            mst = stage.tile([P, TB, H], F32, name="mst%d" % b, tag="mst")
+            msts[b] = mst
+            for i in range(TB):
+                ct, j = where[2][b * TB + i]
+                nc.gpsimd.tensor_tensor(out=mst[:, i, :], in0=ct[:, j * H:(j + 1) * H], in1=lam15[:], op=ALU.mult)
+
+        def mx_m(b):
+            tms[b] = []
+            for j in range(4):
+                am = ps.tile([P, TB * P], F32, name="am%d_%d" % (b, j), tag="ps")
+                for op in range(2):
+                    q, s = qs[(b, op)]
+                    nc.tensor.matmul_mx(out=am[:],
+                                        lhsT=wq[:, op, H + j * P:H + (j + 1) * P].bitcast(FP8X4),
+                                        lhsT_scale=wsc[:, op, H + j * P:H + (j + 1) * P],
+                                        rhs=q[:].bitcast(FP8X4), rhs_scale=s[:],
+                                        start=(op == 0), stop=(op == 1))
+                tm = tpool.tile([P, TB * P], F32, name="tm%d_%d" % (b, j), tag="tm")
+                nc.scalar.activation(out=tm[:], in_=am[:], func=ACT.Tanh, bias=bias_m[:, j:j + 1])
+                tms[b].append(tm)
+
+        gx = t1_in(0, 0, "sv")
+        gh = t1_in(0, 1, "sv")
+        quant_in(gx)
+        gwm0 = t1_w(0, 1)
+        quant_in(gh)
+        gwm1 = t1_w(1, 1)
+        quant_w(gwm0, 0, 1)
+
+        bias_z = const.tile([P, H], F32, name="bias_z")
+        bzp = ps.tile([P, H], F32, name="bzp", tag="ps")
+        nc.tensor.matmul(out=bzp[:], lhsT=ones[:], rhs=vecs[:, 0:H], start=True, stop=True)
+        nc.vector.tensor_copy(out=bias_z[:], in_=bzp[:])
+        lmp = ps.tile([P, H], F32, name="lmp", tag="ps")
+        nc.tensor.matmul(out=lmp[:], lhsT=ones[:], rhs=vecs[:, 2 * H:3 * H], start=True, stop=True)
+        lam = const.tile([P, H], F32, name="lam")
+        nc.scalar.activation(out=lam[:], in_=lmp[:], func=ACT.Exp)
+        lam15 = const.tile([P, H], F32, name="lam15")
+        nc.gpsimd.tensor_scalar(out=lam15[:], in0=lam[:], scalar1=M_SCALE, scalar2=0.0, op0=ALU.mult, op1=ALU.add)
+        pp = ps.tile([P, 4, 32], F32, name="pp", tag="ps")
+        for j in range(4):
+            nc.tensor.matmul(out=pp[:, j, :], lhsT=vecs[:, H + j * P:H + (j + 1) * P], rhs=ones[:, 0:32],
+                             start=True, stop=True)
+        bias_m = const.tile([P, 4], F32, name="bias_m")
+        nc.scalar.copy(out=bias_m[:], in_=pp[:, :, 0])
+        gwz0 = t1_w(0, 0)
+        quant_w(gwm1, 1, 1)
+        gwz1 = t1_w(1, 0)
+        quant_w(gwz0, 0, 0)
+
+        zsts = {}
+        ists = {}
+
+        def final_add(b, lo, hi):
+            nc.vector.tensor_tensor(out=ists[b][:, lo:hi, :], in0=ists[b][:, lo:hi, :], in1=zsts[b][:, lo:hi, :],
+                                    op=ALU.add)
+
+        for b in range(NB + 1):
+            c = b - 1
+            fresh = ()
+            if b + 1 < NB:
+                how = "sv" if b == 0 else "ss"
+                fresh = (t1_in(b + 1, 0, how), t1_in(b + 1, 1, how))
+            if b == 0:
+                quant_w(gwz1, 1, 0)
+                load(0, 24, 4, 0)
+                load(1, 24, 4, 0)
+                load(2, 24, 8, 24)
+                load(0, 28, 4, 4)
+                load(1, 28, 4, 4)
+            if c >= 0:
+                ist = stage.tile([P, TB, H], F32, name="ist%d" % c, tag="ist")
+                ists[c] = ist
+                mst = msts[c]
+                for i in range(TB):
+                    cols = slice(i * P, (i + 1) * P)
+                    tb = ps.tile([P, H], F32, name="tb%d_%d" % (c, i), tag="ps")
+                    for j in range(4):
+                        nc.tensor.transpose(tb[:, j * P:(j + 1) * P], tms[c][j][:, cols], ident[:])
+                    nc.vector.tensor_tensor(out=ist[:, i, :], in0=tb[:], in1=mst[:, i, :], op=ALU.mult)
+                    nc.scalar.mul(out=mst[:, i, :], in_=tb[:], mul=M_SCALE)
+                nc.sync.dma_start(out=dram(outs[1], c * TB, TB), in_=mst[:])
+                if b < NB:
+                    final_add(c, 0, 2)
+                    final_add(c, 2, 4)
+                    nc.sync.dma_start(out=dram(outs[2], c * TB, TB), in_=ist[:])
+                else:
+                    for lo in (0, 2):
+                        final_add(c, lo, lo + 2)
+                        nc.sync.dma_start(out=dram(outs[2], c * TB + lo, 2), in_=ist[:, lo:lo + 2, :])
+            for g in fresh:
+                quant_in(g)
+            if b < NB:
+                scaled_c(b)
+                mx_m(b)
+                zst = stage.tile([P, TB, H], F32, name="zst%d" % b, tag="zst")
+                zsts[b] = zst
+                for i in range(TB):
+                    cols = slice(i * P, (i + 1) * P)
+                    az = ps.tile([P, H], F32, name="az%d_%d" % (b, i), tag="ps")
+                    for op in range(2):
+                        q, s = qs[(b, op)]
+                        nc.tensor.matmul_mx(out=az[:],
+                                            lhsT=q[:, cols].bitcast(FP8X4), lhsT_scale=s[:, cols],
+                                            rhs=wq[:, op, 0:H].bitcast(FP8X4), rhs_scale=wsc[:, op, 0:H],
+                                            start=(op == 0), stop=(op == 1))
+                    nc.vector.tensor_tensor(out=zst[:, i, :], in0=az[:], in1=bias_z[:], op=ALU.add)
+                    nc.scalar.activation(out=zst[:, i, :], in_=zst[:, i, :], func=ACT.Tanh)
+                nc.sync.dma_start(out=dram(outs[0], b * TB, TB), in_=zst[:])

@@ -31,6 +31,7 @@ def tile_koslmcell_pa_t_kernel(tc, x, h_prev, c_prev, W_ih, b_ih, W_hh, b_hh,
         qpool = ctx.enter_context(tc.tile_pool(name="qpool", bufs=3))
         tpool = ctx.enter_context(tc.tile_pool(name="tpool", bufs=8))
         stage = ctx.enter_context(tc.tile_pool(name="stage", bufs=3))
+        ppool = ctx.enter_context(tc.tile_pool(name="ppool", bufs=2))
         ps = ctx.enter_context(tc.psum_pool(name="ps", bufs=8))
         ctx.enter_context(tc.manual_schedule())
 
@@ -89,163 +90,261 @@ def tile_koslmcell_pa_t_kernel(tc, x, h_prev, c_prev, W_ih, b_ih, W_hh, b_hh,
         wq = const.tile([P, 2, 2 * H], U32, name="wq", align_bytes=64)
         wsc = const.tile([P, 2, 2 * H], U8, name="wsc", align_bytes=64)
 
-        def transposes(srcs, label, engines, rows_interleaved=False):
-            grouped = gpool.tile([P, 4 * P, 2], F32, name="grp_" + label, tag="grp", align_bytes=64)
+
+        def permuted(words, label, eng):
+            pm = ppool.tile([P, 4, 2, P], F32, name="pm_" + label, tag="pm")
+            src = words.rearrange("p (a w u) -> p a u w", a=4, u=2)
+            if eng == "v":
+                nc.vector.tensor_copy(out=pm[:], in_=src)
+            else:
+                nc.scalar.copy(out=pm[:], in_=src)
+            return pm
+
+        def t1_pe(srcs, label):
+            banks = []
             for half in range(2):
                 tp = ps.tile([P, 2, 2, P], F32, name="tp_%s_%d" % (label, half), tag="ps")
                 for a in range(2):
                     for u in range(2):
-                        nc.tensor.transpose(tp[:, a, u, :], srcs[2 * half + a][:, u:2 * P:2], ident[:])
-                if rows_interleaved:
-                    dst = grouped[:].rearrange("p (r a) u -> p r a u", a=4)[:, :, 2 * half:2 * half + 2, :]
-                    src = tp[:].rearrange("p a u r -> p r a u")
-                else:
-                    dst = grouped[:, 2 * P * half:2 * P * (half + 1), :].rearrange("p (a r) u -> p a r u", a=2)
-                    src = tp[:].rearrange("p a u r -> p a r u")
-                if engines[half] == "s":
-                    nc.scalar.copy(out=dst, in_=src)
-                else:
-                    nc.vector.tensor_copy(out=dst, in_=src)
-            return grouped
+                        if isinstance(srcs, list):
+                            nc.tensor.transpose(tp[:, a, u, :], srcs[2 * half + a][:, u:2 * P:2], ident[:])
+                        else:
+                            nc.tensor.transpose(tp[:, a, u, :], srcs[:, 2 * half + a, u, :], ident[:])
+                banks.append(tp)
+            return banks
+
+        def t1_copy(banks, grouped, half, eng, inter):
+            tp = banks[half]
+            if inter:
+                dst = grouped[:].rearrange("p (r a) u -> p r a u", a=4)[:, :, 2 * half:2 * half + 2, :]
+                src = tp[:].rearrange("p a u r -> p r a u")
+            else:
+                dst = grouped[:, 2 * P * half:2 * P * (half + 1), :].rearrange("p (a r) u -> p a r u", a=2)
+                src = tp[:].rearrange("p a u r -> p a r u")
+            if eng == "s":
+                nc.scalar.copy(out=dst, in_=src)
+            else:
+                nc.vector.tensor_copy(out=dst, in_=src)
+
+        def new_grp(label):
+            return gpool.tile([P, 4 * P, 2], F32, name="grp_" + label, tag="grp", align_bytes=64)
 
         def quantise(grouped, codes, scales):
             nc.vector.quantize_mx(out=codes.bitcast(FP8X4), scales=scales,
                                   in_=grouped[:].rearrange("p c u -> p (c u)").bitcast(BF16))
 
-        def t1_w(op, half):
+        st = {}
+        qs = {}
+
+        def w_srcs(op, half):
             wv = wraw[(op, half)][:].bitcast(F32)
-            srcs = [wv[:, a * (D // 2):(a + 1) * (D // 2)] for a in range(4)]
-            return transposes(srcs, "w%d%d" % (op, half), ("ss", "vv")[op], rows_interleaved=True)
+            return [wv[:, a * (D // 2):(a + 1) * (D // 2)] for a in range(4)]
 
-        def quant_w(g, op, half):
-            quantise(g, wq[:, op, half * H:(half + 1) * H], wsc[:, op, half * H:(half + 1) * H])
-
-        def t1_in(b, op, engines):
+        def in_srcs(o):
+            b, op = divmod(o, 2)
             srcs = []
             for t in range(b * TB, (b + 1) * TB):
                 rt, j = where[op][t]
                 srcs.append(rt[:].bitcast(F32)[:, j * (D // 2):(j + 1) * (D // 2)])
-            return (transposes(srcs, "b%d_%d" % (b, op), engines), b, op)
+            return srcs
 
-        qs = {}
+        def ev_T1pp(o, eng):
+            b, op = divmod(o, 2)
+            rt, j = where[op][b * TB]
+            st[("pm", o)] = permuted(rt[:].bitcast(F32)[:, j * (D // 2):(j + 4) * (D // 2)], "i%d" % o, eng)
 
-        def quant_in(gbo):
-            g, b, op = gbo
-            q = qpool.tile([P, TB * P], U32, name="q%d_%d" % (b, op), tag="q%d" % op, align_bytes=64)
-            s = qpool.tile([P, TB * P], U8, name="s%d_%d" % (b, op), tag="s%d" % op, align_bytes=64)
-            quantise(g, q[:], s[:])
-            qs[(b, op)] = (q, s)
+        def ev_T1pt(o):
+            st[("t1", o)] = t1_pe(st[("pm", o)], "i%d" % o)
 
-        tms = {}
-        msts = {}
+        def w_T1pp(op, half, eng):
+            st[("wpm", op, half)] = permuted(wraw[(op, half)][:].bitcast(F32), "w%d%d" % (op, half), eng)
 
-        def scaled_c(b):
-            mst = stage.tile([P, TB, H], F32, name="mst%d" % b, tag="mst")
-            msts[b] = mst
-            for i in range(TB):
-                ct, j = where[2][b * TB + i]
-                nc.gpsimd.tensor_tensor(out=mst[:, i, :], in0=ct[:, j * H:(j + 1) * H], in1=lam15[:], op=ALU.mult)
+        def w_T1pt(op, half):
+            st[("wt1", op, half)] = t1_pe(st[("wpm", op, half)], "w%d%d" % (op, half))
 
-        def mx_m(b):
-            tms[b] = []
+        def ev_T1p(o):
+            st[("t1", o)] = t1_pe(in_srcs(o), "i%d" % o)
+
+        def ev_T1c(o, engs):
+            g = new_grp("i%d" % o)
+            st[("g", o)] = g
+            for half in range(2):
+                t1_copy(st[("t1", o)], g, half, engs[half], False)
+
+        def ev_Q(o):
+            b, op = divmod(o, 2)
+            q = qpool.tile([P, TB * P], U32, name="q%d" % o, tag="q%d" % op, align_bytes=64)
+            s = qpool.tile([P, TB * P], U8, name="s%d" % o, tag="s%d" % op, align_bytes=64)
+            quantise(st[("g", o)], q[:], s[:])
+            qs[o] = (q, s)
+
+        def w_T1p(op, half):
+            st[("wt1", op, half)] = t1_pe(w_srcs(op, half), "w%d%d" % (op, half))
+
+        def w_T1c(op, half, engs):
+            g = new_grp("w%d%d" % (op, half))
+            st[("wg", op, half)] = g
+            for h2 in range(2):
+                t1_copy(st[("wt1", op, half)], g, h2, engs[h2], True)
+
+        def w_Q(op, half):
+            quantise(st[("wg", op, half)], wq[:, op, half * H:(half + 1) * H], wsc[:, op, half * H:(half + 1) * H])
+
+        msts, zsts, ists = {}, {}, {}
+
+        def ev_CS(b, i):
+            if i == 0:
+                msts[b] = stage.tile([P, TB, H], F32, name="mst%d" % b, tag="mst")
+            ct, j = where[2][b * TB + i]
+            nc.gpsimd.tensor_tensor(out=msts[b][:, i, :], in0=ct[:, j * H:(j + 1) * H], in1=lam15[:], op=ALU.mult)
+
+        def ev_AMp(b, j):
+            am = ps.tile([P, TB * P], F32, name="am%d_%d" % (b, j), tag="ps")
+            for op in range(2):
+                q, s = qs[2 * b + op]
+                nc.tensor.matmul_mx(out=am[:], lhsT=wq[:, op, H + j * P:H + (j + 1) * P].bitcast(FP8X4),
+                                    lhsT_scale=wsc[:, op, H + j * P:H + (j + 1) * P],
+                                    rhs=q[:].bitcast(FP8X4), rhs_scale=s[:], start=(op == 0), stop=(op == 1))
+            st[("am", b, j)] = am
+
+        def ev_AMs(b, j):
+            tm = tpool.tile([P, TB * P], F32, name="tm%d_%d" % (b, j), tag="tm")
+            nc.scalar.activation(out=tm[:], in_=st[("am", b, j)][:], func=ACT.Tanh, bias=bias_m[:, j:j + 1])
+            st[("tm", b, j)] = tm
+
+        def ev_AZp(b, i):
+            if i == 0:
+                zsts[b] = stage.tile([P, TB, H], F32, name="zst%d" % b, tag="zst")
+            cols = slice(i * P, (i + 1) * P)
+            az = ps.tile([P, H], F32, name="az%d_%d" % (b, i), tag="ps")
+            for op in range(2):
+                q, s = qs[2 * b + op]
+                nc.tensor.matmul_mx(out=az[:], lhsT=q[:, cols].bitcast(FP8X4), lhsT_scale=s[:, cols],
+                                    rhs=wq[:, op, 0:H].bitcast(FP8X4), rhs_scale=wsc[:, op, 0:H],
+                                    start=(op == 0), stop=(op == 1))
+            st[("az", b, i)] = az
+
+        def ev_AZv(b, i):
+            nc.vector.tensor_tensor(out=zsts[b][:, i, :], in0=st[("az", b, i)][:], in1=bias_z[:], op=ALU.add)
+
+        def ev_AZs(b, i):
+            nc.scalar.activation(out=zsts[b][:, i, :], in_=zsts[b][:, i, :], func=ACT.Tanh)
+
+        def ev_TBp(c, i):
+            if i == 0:
+                ists[c] = stage.tile([P, TB, H], F32, name="ist%d" % c, tag="ist")
+            cols = slice(i * P, (i + 1) * P)
+            tb = ps.tile([P, H], F32, name="tb%d_%d" % (c, i), tag="ps")
             for j in range(4):
-                am = ps.tile([P, TB * P], F32, name="am%d_%d" % (b, j), tag="ps")
-                for op in range(2):
-                    q, s = qs[(b, op)]
-                    nc.tensor.matmul_mx(out=am[:],
-                                        lhsT=wq[:, op, H + j * P:H + (j + 1) * P].bitcast(FP8X4),
-                                        lhsT_scale=wsc[:, op, H + j * P:H + (j + 1) * P],
-                                        rhs=q[:].bitcast(FP8X4), rhs_scale=s[:],
-                                        start=(op == 0), stop=(op == 1))
-                tm = tpool.tile([P, TB * P], F32, name="tm%d_%d" % (b, j), tag="tm")
-                nc.scalar.activation(out=tm[:], in_=am[:], func=ACT.Tanh, bias=bias_m[:, j:j + 1])
-                tms[b].append(tm)
+                nc.tensor.transpose(tb[:, j * P:(j + 1) * P], st[("tm", c, j)][:, cols], ident[:])
+            st[("tb", c, i)] = tb
 
-        gx = t1_in(0, 0, "sv")
-        gh = t1_in(0, 1, "sv")
-        quant_in(gx)
-        gwm0 = t1_w(0, 1)
-        quant_in(gh)
-        gwm1 = t1_w(1, 1)
-        quant_w(gwm0, 0, 1)
+        def ev_TBv(c, i):
+            nc.vector.tensor_tensor(out=ists[c][:, i, :], in0=st[("tb", c, i)][:], in1=msts[c][:, i, :], op=ALU.mult)
+
+        def ev_TBs(c, i):
+            nc.scalar.mul(out=msts[c][:, i, :], in_=st[("tb", c, i)][:], mul=M_SCALE)
+
+        def ev_FA(c, i, n):
+            nc.vector.tensor_tensor(out=ists[c][:, i:i + n, :], in0=ists[c][:, i:i + n, :], in1=zsts[c][:, i:i + n, :], op=ALU.add)
+
+        def ev_STm(c, i, n):
+            nc.sync.dma_start(out=dram(outs[1], c * TB + i, n), in_=msts[c][:, i:i + n, :])
+
+        def ev_STi(c, i, n):
+            nc.sync.dma_start(out=dram(outs[2], c * TB + i, n), in_=ists[c][:, i:i + n, :])
+
+        def ev_STz(c, i, n):
+            nc.sync.dma_start(out=dram(outs[0], c * TB + i, n), in_=zsts[c][:, i:i + n, :])
+
 
         bias_z = const.tile([P, H], F32, name="bias_z")
-        bzp = ps.tile([P, H], F32, name="bzp", tag="ps")
-        nc.tensor.matmul(out=bzp[:], lhsT=ones[:], rhs=vecs[:, 0:H], start=True, stop=True)
-        nc.vector.tensor_copy(out=bias_z[:], in_=bzp[:])
-        lmp = ps.tile([P, H], F32, name="lmp", tag="ps")
-        nc.tensor.matmul(out=lmp[:], lhsT=ones[:], rhs=vecs[:, 2 * H:3 * H], start=True, stop=True)
         lam = const.tile([P, H], F32, name="lam")
-        nc.scalar.activation(out=lam[:], in_=lmp[:], func=ACT.Exp)
         lam15 = const.tile([P, H], F32, name="lam15")
-        nc.gpsimd.tensor_scalar(out=lam15[:], in0=lam[:], scalar1=M_SCALE, scalar2=0.0, op0=ALU.mult, op1=ALU.add)
-        pp = ps.tile([P, 4, 32], F32, name="pp", tag="ps")
-        for j in range(4):
-            nc.tensor.matmul(out=pp[:, j, :], lhsT=vecs[:, H + j * P:H + (j + 1) * P], rhs=ones[:, 0:32],
-                             start=True, stop=True)
         bias_m = const.tile([P, 4], F32, name="bias_m")
-        nc.scalar.copy(out=bias_m[:], in_=pp[:, :, 0])
-        gwz0 = t1_w(0, 0)
-        quant_w(gwm1, 1, 1)
-        gwz1 = t1_w(1, 0)
-        quant_w(gwz0, 0, 0)
+        def vec_bits():
+            bzp = ps.tile([P, H], F32, name="bzp", tag="ps")
+            nc.tensor.matmul(out=bzp[:], lhsT=ones[:], rhs=vecs[:, 0:H], start=True, stop=True)
+            nc.vector.tensor_copy(out=bias_z[:], in_=bzp[:])
+            lmp = ps.tile([P, H], F32, name="lmp", tag="ps")
+            nc.tensor.matmul(out=lmp[:], lhsT=ones[:], rhs=vecs[:, 2 * H:3 * H], start=True, stop=True)
+            nc.scalar.activation(out=lam[:], in_=lmp[:], func=ACT.Exp)
+            nc.gpsimd.tensor_scalar(out=lam15[:], in0=lam[:], scalar1=M_SCALE, scalar2=0.0, op0=ALU.mult, op1=ALU.add)
+            pp = ps.tile([P, 4, 32], F32, name="pp", tag="ps")
+            for j in range(4):
+                nc.tensor.matmul(out=pp[:, j, :], lhsT=vecs[:, H + j * P:H + (j + 1) * P], rhs=ones[:, 0:32],
+                                 start=True, stop=True)
+            nc.scalar.copy(out=bias_m[:], in_=pp[:, :, 0])
+        def T1(o, engs):
+            ev_T1p(o)
+            ev_T1c(o, engs)
+        def WT1(op, half, engs):
+            w_T1p(op, half)
+            w_T1c(op, half, engs)
 
-        zsts = {}
-        ists = {}
-
-        def final_add(b, lo, hi):
-            nc.vector.tensor_tensor(out=ists[b][:, lo:hi, :], in0=ists[b][:, lo:hi, :], in1=zsts[b][:, lo:hi, :],
-                                    op=ALU.add)
-
+        ev_T1pp(0, "v")
+        ev_T1pp(1, "v")
+        ev_T1pt(0)
+        ev_T1c(0, "sv")
+        w_T1pp(0, 1, "v")
+        ev_Q(0)
+        ev_T1pt(1)
+        ev_T1c(1, "sv")
+        w_T1pp(1, 1, "v")
+        ev_Q(1)
+        w_T1pt(0, 1)
+        w_T1c(0, 1, "ss")
+        w_T1pp(0, 0, "v")
+        w_Q(0, 1)
+        w_T1pt(1, 1)
+        w_T1c(1, 1, "ss")
+        w_T1pp(1, 0, "v")
+        w_Q(1, 1)
+        vec_bits()
+        w_T1pt(0, 0)
+        w_T1c(0, 0, "sv")
+        w_Q(0, 0)
+        w_T1pt(1, 0)
+        w_T1c(1, 0, "sv")
+        w_Q(1, 0)
         for b in range(NB + 1):
             c = b - 1
-            fresh = ()
-            if b + 1 < NB:
-                how = "sv" if b == 0 else "ss"
-                fresh = (t1_in(b + 1, 0, how), t1_in(b + 1, 1, how))
+            o = 2 * b + 2
+            if b < NB:
+                for i in range(4):
+                    ev_CS(b, i)
+            for h in range(2):
+                if o + h < 2 * NB:
+                    T1(o + h, "sv" if b == 0 else "ss")
+                    if b == 0:
+                        load(h, 24, 4, 0)
+                if c >= 0:
+                    for i in (2 * h, 2 * h + 1):
+                        ev_TBp(c, i)
+                        ev_TBv(c, i)
+                        ev_TBs(c, i)
+                    if b == NB:
+                        ev_STm(c, 2 * h, 2)
+                        ev_FA(c, 2 * h, 2)
+                        ev_STi(c, 2 * h, 2)
             if b == 0:
-                quant_w(gwz1, 1, 0)
-                load(0, 24, 4, 0)
-                load(1, 24, 4, 0)
                 load(2, 24, 8, 24)
                 load(0, 28, 4, 4)
                 load(1, 28, 4, 4)
-            if c >= 0:
-                ist = stage.tile([P, TB, H], F32, name="ist%d" % c, tag="ist")
-                ists[c] = ist
-                mst = msts[c]
-                for i in range(TB):
-                    cols = slice(i * P, (i + 1) * P)
-                    tb = ps.tile([P, H], F32, name="tb%d_%d" % (c, i), tag="ps")
-                    for j in range(4):
-                        nc.tensor.transpose(tb[:, j * P:(j + 1) * P], tms[c][j][:, cols], ident[:])
-                    nc.vector.tensor_tensor(out=ist[:, i, :], in0=tb[:], in1=mst[:, i, :], op=ALU.mult)
-                    nc.scalar.mul(out=mst[:, i, :], in_=tb[:], mul=M_SCALE)
-                nc.sync.dma_start(out=dram(outs[1], c * TB, TB), in_=mst[:])
-                if b < NB:
-                    final_add(c, 0, 2)
-                    final_add(c, 2, 4)
-                    nc.sync.dma_start(out=dram(outs[2], c * TB, TB), in_=ist[:])
-                else:
-                    for lo in (0, 2):
-                        final_add(c, lo, lo + 2)
-                        nc.sync.dma_start(out=dram(outs[2], c * TB + lo, 2), in_=ist[:, lo:lo + 2, :])
-            for g in fresh:
-                quant_in(g)
             if b < NB:
-                scaled_c(b)
-                mx_m(b)
-                zst = stage.tile([P, TB, H], F32, name="zst%d" % b, tag="zst")
-                zsts[b] = zst
-                for i in range(TB):
-                    cols = slice(i * P, (i + 1) * P)
-                    az = ps.tile([P, H], F32, name="az%d_%d" % (b, i), tag="ps")
-                    for op in range(2):
-                        q, s = qs[(b, op)]
-                        nc.tensor.matmul_mx(out=az[:],
-                                            lhsT=q[:, cols].bitcast(FP8X4), lhsT_scale=s[:, cols],
-                                            rhs=wq[:, op, 0:H].bitcast(FP8X4), rhs_scale=wsc[:, op, 0:H],
-                                            start=(op == 0), stop=(op == 1))
-                    nc.vector.tensor_tensor(out=zst[:, i, :], in0=az[:], in1=bias_z[:], op=ALU.add)
-                    nc.scalar.activation(out=zst[:, i, :], in_=zst[:, i, :], func=ACT.Tanh)
-                nc.sync.dma_start(out=dram(outs[0], b * TB, TB), in_=zst[:])
+                if c >= 0:
+                    ev_STm(c, 0, TB)
+                    ev_FA(c, 0, 2)
+                    ev_FA(c, 2, 2)
+                    ev_STi(c, 0, TB)
+                for h in range(2):
+                    if o + h < 2 * NB:
+                        ev_Q(o + h)
+                for j in range(4):
+                    ev_AMp(b, j)
+                    ev_AMs(b, j)
+                for i in range(4):
+                    ev_AZp(b, i)
+                    ev_AZv(b, i)
+                    ev_AZs(b, i)
+                ev_STz(b, 0, TB)

@@ -31,7 +31,7 @@ def tile_koslmcell_pa_t_kernel(tc, x, h_prev, c_prev, W_ih, b_ih, W_hh, b_hh,
         qpool = ctx.enter_context(tc.tile_pool(name="qpool", bufs=3))
         tpool = ctx.enter_context(tc.tile_pool(name="tpool", bufs=8))
         stage = ctx.enter_context(tc.tile_pool(name="stage", bufs=3))
-        ppool = ctx.enter_context(tc.tile_pool(name="ppool", bufs=2))
+        mstp = ctx.enter_context(tc.tile_pool(name="mstp", bufs=4))
         ps = ctx.enter_context(tc.psum_pool(name="ps", bufs=8))
         ctx.enter_context(tc.manual_schedule())
 
@@ -92,7 +92,7 @@ def tile_koslmcell_pa_t_kernel(tc, x, h_prev, c_prev, W_ih, b_ih, W_hh, b_hh,
 
 
         def permuted(words, label, eng):
-            pm = ppool.tile([P, 4, 2, P], F32, name="pm_" + label, tag="pm")
+            pm = gpool.tile([P, 4, 2, P], F32, name="pm_" + label, tag="grp", align_bytes=64)
             src = words.rearrange("p (a w u) -> p a u w", a=4, u=2)
             if eng == "v":
                 nc.vector.tensor_copy(out=pm[:], in_=src)
@@ -194,7 +194,7 @@ def tile_koslmcell_pa_t_kernel(tc, x, h_prev, c_prev, W_ih, b_ih, W_hh, b_hh,
 
         def ev_CS(b, i):
             if i == 0:
-                msts[b] = stage.tile([P, TB, H], F32, name="mst%d" % b, tag="mst")
+                msts[b] = mstp.tile([P, TB, H], F32, name="mst%d" % b, tag="mst")
             ct, j = where[2][b * TB + i]
             nc.gpsimd.tensor_tensor(out=msts[b][:, i, :], in0=ct[:, j * H:(j + 1) * H], in1=lam15[:], op=ALU.mult)
 
@@ -248,6 +248,27 @@ def tile_koslmcell_pa_t_kernel(tc, x, h_prev, c_prev, W_ih, b_ih, W_hh, b_hh,
         def ev_FA(c, i, n):
             nc.vector.tensor_tensor(out=ists[c][:, i:i + n, :], in0=ists[c][:, i:i + n, :], in1=zsts[c][:, i:i + n, :], op=ALU.add)
 
+        def ev_FAg(c, i):
+            nc.gpsimd.tensor_tensor(out=ists[c][:, i, :], in0=ists[c][:, i, :], in1=zsts[c][:, i, :], op=ALU.add)
+
+        def ev_trig():
+            nc.vector.tensor_copy(out=lamg[:, 0:1], in_=lam15[:, 0:1])
+
+        def ev_CS1(b, i, eng):
+            if b not in msts:
+                msts[b] = mstp.tile([P, TB, H], F32, name="mst%d" % b, tag="mst")
+            ct, j = where[2][b * TB + i]
+            if eng == "g":
+                nc.gpsimd.tensor_tensor(out=msts[b][:, i, :], in0=ct[:, j * H:(j + 1) * H], in1=lamg[:], op=ALU.mult)
+            else:
+                nc.vector.tensor_tensor(out=msts[b][:, i, :], in0=ct[:, j * H:(j + 1) * H], in1=lam15[:], op=ALU.mult)
+
+        def ev_CSv(b, i):
+            if i == 0:
+                msts[b] = mstp.tile([P, TB, H], F32, name="mst%d" % b, tag="mst")
+            ct, j = where[2][b * TB + i]
+            nc.vector.tensor_tensor(out=msts[b][:, i, :], in0=ct[:, j * H:(j + 1) * H], in1=lam15[:], op=ALU.mult)
+
         def ev_STm(c, i, n):
             nc.sync.dma_start(out=dram(outs[1], c * TB + i, n), in_=msts[c][:, i:i + n, :])
 
@@ -261,6 +282,7 @@ def tile_koslmcell_pa_t_kernel(tc, x, h_prev, c_prev, W_ih, b_ih, W_hh, b_hh,
         bias_z = const.tile([P, H], F32, name="bias_z")
         lam = const.tile([P, H], F32, name="lam")
         lam15 = const.tile([P, H], F32, name="lam15")
+        lamg = const.tile([P, H], F32, name="lamg")
         bias_m = const.tile([P, 4], F32, name="bias_m")
         def vec_bits():
             bzp = ps.tile([P, H], F32, name="bzp", tag="ps")
@@ -270,6 +292,7 @@ def tile_koslmcell_pa_t_kernel(tc, x, h_prev, c_prev, W_ih, b_ih, W_hh, b_hh,
             nc.tensor.matmul(out=lmp[:], lhsT=ones[:], rhs=vecs[:, 2 * H:3 * H], start=True, stop=True)
             nc.scalar.activation(out=lam[:], in_=lmp[:], func=ACT.Exp)
             nc.gpsimd.tensor_scalar(out=lam15[:], in0=lam[:], scalar1=M_SCALE, scalar2=0.0, op0=ALU.mult, op1=ALU.add)
+            nc.gpsimd.tensor_scalar(out=lamg[:], in0=lam[:], scalar1=M_SCALE, scalar2=0.0, op0=ALU.mult, op1=ALU.add)
             pp = ps.tile([P, 4, 32], F32, name="pp", tag="ps")
             for j in range(4):
                 nc.tensor.matmul(out=pp[:, j, :], lhsT=vecs[:, H + j * P:H + (j + 1) * P], rhs=ones[:, 0:32],
@@ -307,12 +330,12 @@ def tile_koslmcell_pa_t_kernel(tc, x, h_prev, c_prev, W_ih, b_ih, W_hh, b_hh,
         w_T1pt(1, 0)
         w_T1c(1, 0, "sv")
         w_Q(1, 0)
+
+        for i in range(4):
+            ev_CS1(0, i, "g")
         for b in range(NB + 1):
             c = b - 1
             o = 2 * b + 2
-            if b < NB:
-                for i in range(4):
-                    ev_CS(b, i)
             for h in range(2):
                 if o + h < 2 * NB:
                     T1(o + h, "sv" if b == 0 else "ss")
@@ -334,12 +357,25 @@ def tile_koslmcell_pa_t_kernel(tc, x, h_prev, c_prev, W_ih, b_ih, W_hh, b_hh,
             if b < NB:
                 if c >= 0:
                     ev_STm(c, 0, TB)
-                    ev_FA(c, 0, 2)
-                    ev_FA(c, 2, 2)
-                    ev_STi(c, 0, TB)
-                for h in range(2):
-                    if o + h < 2 * NB:
-                        ev_Q(o + h)
+                def fa():
+                    if c >= 0:
+                        ev_FA(c, 0, 2)
+                        ev_FA(c, 2, 2)
+                        ev_STi(c, 0, TB)
+                def cs():
+                    if b + 1 < NB:
+                        for i in range(0):
+                            ev_CS1(b + 1, i, "v")
+                def qq():
+                    for h in range(2):
+                        if o + h < 2 * NB:
+                            ev_Q(o + h)
+                for k in "FCQ":
+                    (fa if k == "F" else cs if k == "C" else qq)()
+                ev_trig()
+                if b + 1 < NB:
+                    for i in range(0, 4):
+                        ev_CS1(b + 1, i, "g")
                 for j in range(4):
                     ev_AMp(b, j)
                     ev_AMs(b, j)

@@ -38,6 +38,9 @@ def tile_koslmcell_pa_t_kernel(tc, x, h_prev, c_prev, W_ih, b_ih, W_hh, b_hh,
         def row(v):
             return v.rearrange("(o n) -> o n", o=1)
 
+        warm = const.tile([P, 2], F32, name="warm")
+        nc.vector.memset(warm[:], 0.0)
+        nc.scalar.activation(out=warm[:, 1:2], in_=warm[:, 0:1], func=ACT.Tanh)
         vecs = const.tile([P, 3 * H], BF16, name="vecs")
         nc.vector.memset(vecs[:], 0.0)
         ones = const.tile([P, P], BF16, name="ones")
@@ -338,7 +341,7 @@ def tile_koslmcell_pa_t_kernel(tc, x, h_prev, c_prev, W_ih, b_ih, W_hh, b_hh,
             o = 2 * b + 2
             for h in range(2):
                 if o + h < 2 * NB:
-                    T1(o + h, "sv" if b == 0 else "ss")
+                    T1(o + h, "sv" if b == 0 else ("ss", "sv")[h])
                     if b == 0:
                         load(h, 24, 4, 0)
                 if c >= 0:

@@ -45,11 +45,6 @@ def tile_koslmcell_pa_t_kernel(tc, x, h_prev, c_prev, W_ih, b_ih, W_hh, b_hh,
         nc.vector.memset(vecs[:], 0.0)
         ones = const.tile([P, P], BF16, name="ones")
         nc.vector.memset(ones[:], 1.0)
-        nc.scalar.dma_start(out=vecs[0:1, 0:2 * H], in_=row(b_ih))
-        nc.scalar.dma_start(out=vecs[1:2, 0:2 * H], in_=row(b_hh))
-        nc.scalar.dma_start(out=vecs[2:3, 0:H], in_=row(z_bias))
-        nc.scalar.dma_start(out=vecs[2:3, H:2 * H], in_=row(m_bias))
-        nc.scalar.dma_start(out=vecs[0:1, 2 * H:3 * H], in_=row(log_lambda))
         ident = const.tile([P, P], F32, name="ident")
         make_identity(nc, ident[:])
 
@@ -79,15 +74,20 @@ def tile_koslmcell_pa_t_kernel(tc, x, h_prev, c_prev, W_ih, b_ih, W_hh, b_hh,
         wraw[(1, 1)] = load_w(1, 1, "ist")
         wraw[(0, 0)] = load_w(0, 0, "zst")
         wraw[(1, 0)] = load_w(1, 0, "ist")
+        nc.scalar.dma_start(out=vecs[0:1, 0:2 * H], in_=row(b_ih))
+        nc.scalar.dma_start(out=vecs[1:2, 0:2 * H], in_=row(b_hh))
+        nc.scalar.dma_start(out=vecs[2:3, 0:H], in_=row(z_bias))
+        nc.scalar.dma_start(out=vecs[2:3, H:2 * H], in_=row(m_bias))
+        nc.scalar.dma_start(out=vecs[0:1, 2 * H:3 * H], in_=row(log_lambda))
         load(0, 4, 4, 4)
         load(1, 4, 4, 4)
         load(2, 0, 4, 0)
+        load(2, 4, 4, 4)
         load(0, 8, 8, 8)
         load(1, 8, 8, 8)
-        load(2, 4, 4, 4)
+        load(2, 8, 8, 8)
         load(0, 16, 8, 16)
         load(1, 16, 8, 16)
-        load(2, 8, 8, 8)
         load(2, 16, 8, 16)
 
         wq = const.tile([P, 2, 2 * H], U32, name="wq", align_bytes=64)
@@ -248,6 +248,9 @@ def tile_koslmcell_pa_t_kernel(tc, x, h_prev, c_prev, W_ih, b_ih, W_hh, b_hh,
         def ev_TBs(c, i):
             nc.scalar.mul(out=msts[c][:, i, :], in_=st[("tb", c, i)][:], mul=M_SCALE)
 
+        def ev_TBsv(c, i):
+            nc.vector.tensor_scalar(out=msts[c][:, i, :], in0=st[("tb", c, i)][:], scalar1=M_SCALE, scalar2=0.0, op0=ALU.mult, op1=ALU.add)
+
         def ev_FA(c, i, n):
             nc.vector.tensor_tensor(out=ists[c][:, i:i + n, :], in0=ists[c][:, i:i + n, :], in1=zsts[c][:, i:i + n, :], op=ALU.add)
 
@@ -334,25 +337,35 @@ def tile_koslmcell_pa_t_kernel(tc, x, h_prev, c_prev, W_ih, b_ih, W_hh, b_hh,
         w_T1c(1, 0, "sv")
         w_Q(1, 0)
 
-        for i in range(4):
-            ev_CS1(0, i, "g")
+        def nv(b):
+            return 4 if b == 0 else 1 if b == 1 else (1 if b % 2 else 0)
         for b in range(NB + 1):
             c = b - 1
             o = 2 * b + 2
             for h in range(2):
                 if o + h < 2 * NB:
-                    T1(o + h, "sv" if b == 0 else ("ss", "sv")[h])
+                    T1(o + h, ("ss", "ss")[h] if b == 0 else ("ss", "ss" if b % 2 else "sv")[h])
                     if b == 0:
                         load(h, 24, 4, 0)
                 if c >= 0:
                     for i in (2 * h, 2 * h + 1):
                         ev_TBp(c, i)
                         ev_TBv(c, i)
-                        ev_TBs(c, i)
+                        if b == NB and i in ():
+                            ev_TBsv(c, i)
+                        else:
+                            ev_TBs(c, i)
                     if b == NB:
                         ev_STm(c, 2 * h, 2)
-                        ev_FA(c, 2 * h, 2)
-                        ev_STi(c, 2 * h, 2)
+                        if h == 0:
+                            for i in (0,):
+                                ev_FAg(c, i)
+                        else:
+                            for i in range(4):
+                                if i not in (0,):
+                                    ev_FA(c, i, 1)
+                                if i in (1, 3):
+                                    ev_STi(c, i - 1, 2)
             if b == 0:
                 load(2, 24, 8, 24)
                 load(0, 28, 4, 4)
@@ -360,25 +373,21 @@ def tile_koslmcell_pa_t_kernel(tc, x, h_prev, c_prev, W_ih, b_ih, W_hh, b_hh,
             if b < NB:
                 if c >= 0:
                     ev_STm(c, 0, TB)
-                def fa():
-                    if c >= 0:
-                        ev_FA(c, 0, 2)
-                        ev_FA(c, 2, 2)
-                        ev_STi(c, 0, TB)
-                def cs():
-                    if b + 1 < NB:
-                        for i in range(0):
-                            ev_CS1(b + 1, i, "v")
-                def qq():
-                    for h in range(2):
-                        if o + h < 2 * NB:
-                            ev_Q(o + h)
-                for k in "FCQ":
-                    (fa if k == "F" else cs if k == "C" else qq)()
+                    ev_FA(c, 0, 2)
+                    ev_FA(c, 2, 2)
+                    ev_STi(c, 0, TB)
+                for b2 in ((0, 1) if b == 0 else (b + 1,)):
+                    if b2 < NB:
+                        for i in range(nv(b2)):
+                            ev_CS1(b2, i, "v")
+                for h in range(2):
+                    if o + h < 2 * NB:
+                        ev_Q(o + h)
                 ev_trig()
-                if b + 1 < NB:
-                    for i in range(0, 4):
-                        ev_CS1(b + 1, i, "g")
+                for b2 in ((0, 1) if b == 0 else (b + 1,)):
+                    if b2 < NB:
+                        for i in range(nv(b2), 4):
+                            ev_CS1(b2, i, "g")
                 for j in range(4):
                     ev_AMp(b, j)
                     ev_AMs(b, j)

@@ -28,9 +28,11 @@ def tile_koslmcell_pa_t_kernel(tc, x, h_prev, c_prev, W_ih, b_ih, W_hh, b_hh,
         const = ctx.enter_context(tc.tile_pool(name="const", bufs=1))
         resid = ctx.enter_context(tc.tile_pool(name="resid", bufs=1))
         gpool = ctx.enter_context(tc.tile_pool(name="gpool", bufs=4))
-        qpool = ctx.enter_context(tc.tile_pool(name="qpool", bufs=3))
+        qpool = ctx.enter_context(tc.tile_pool(name="qpool", bufs=1))
         tpool = ctx.enter_context(tc.tile_pool(name="tpool", bufs=8))
         stage = ctx.enter_context(tc.tile_pool(name="stage", bufs=3))
+        g2pool = ctx.enter_context(tc.tile_pool(name="g2pool", bufs=2))
+        q2pool = ctx.enter_context(tc.tile_pool(name="q2pool", bufs=3))
         mstp = ctx.enter_context(tc.tile_pool(name="mstp", bufs=4))
         ps = ctx.enter_context(tc.psum_pool(name="ps", bufs=8))
         ctx.enter_context(tc.manual_schedule())
@@ -61,28 +63,35 @@ def tile_koslmcell_pa_t_kernel(tc, x, h_prev, c_prev, W_ih, b_ih, W_hh, b_hh,
             for j in range(n):
                 where[i][t0 + j] = (rt, j)
 
+        def load_half(i, t0, rt, j0, n):
+            nc.sync.dma_start(out=rt[:, j0 * D:(j0 + n) * D].rearrange("p (t k) -> p t k", k=D), in_=dram(views[i], t0, n))
+            for j in range(n):
+                where[i][t0 + j] = (rt, j0 + j)
+
         def load_w(op, half, tag):
             w = (W_ih, W_hh)[op]
             wr = stage.tile([P, 4 * D], BF16, name="wraw%d%d" % (op, half), tag=tag)
             nc.sync.dma_start(out=wr[:], in_=w[half * H:(half + 1) * H, :].rearrange("(p a) k -> p (a k)", a=4))
             return wr
 
-        load(0, 0, 4, 0)
-        load(1, 0, 4, 0)
+        first = {}
+        for i in range(2):
+            first[i] = resid.tile([P, 8 * D], BF16, name="in%d_0" % i, tag="%s0" % "xh"[i])
+        load_half(0, 0, first[0], 0, 4)
+        load_half(1, 0, first[1], 0, 4)
         wraw = {}
         wraw[(0, 1)] = load_w(0, 1, "zst")
         wraw[(1, 1)] = load_w(1, 1, "ist")
+        nc.sync.dma_start(out=vecs[0:1, 0:2 * H], in_=row(b_ih))
+        nc.sync.dma_start(out=vecs[1:2, 0:2 * H], in_=row(b_hh))
+        nc.sync.dma_start(out=vecs[2:3, 0:H], in_=row(z_bias))
+        nc.sync.dma_start(out=vecs[2:3, H:2 * H], in_=row(m_bias))
+        nc.sync.dma_start(out=vecs[0:1, 2 * H:3 * H], in_=row(log_lambda))
         wraw[(0, 0)] = load_w(0, 0, "zst")
         wraw[(1, 0)] = load_w(1, 0, "ist")
-        nc.scalar.dma_start(out=vecs[0:1, 0:2 * H], in_=row(b_ih))
-        nc.scalar.dma_start(out=vecs[1:2, 0:2 * H], in_=row(b_hh))
-        nc.scalar.dma_start(out=vecs[2:3, 0:H], in_=row(z_bias))
-        nc.scalar.dma_start(out=vecs[2:3, H:2 * H], in_=row(m_bias))
-        nc.scalar.dma_start(out=vecs[0:1, 2 * H:3 * H], in_=row(log_lambda))
-        load(0, 4, 4, 4)
-        load(1, 4, 4, 4)
-        load(2, 0, 4, 0)
-        load(2, 4, 4, 4)
+        load_half(0, 4, first[0], 4, 4)
+        load_half(1, 4, first[1], 4, 4)
+        load(2, 0, 8, 0)
         load(0, 8, 8, 8)
         load(1, 8, 8, 8)
         load(2, 8, 8, 8)
@@ -128,6 +137,35 @@ def tile_koslmcell_pa_t_kernel(tc, x, h_prev, c_prev, W_ih, b_ih, W_hh, b_hh,
                 nc.scalar.copy(out=dst, in_=src)
             else:
                 nc.vector.tensor_copy(out=dst, in_=src)
+
+        def new_grp2(label):
+            return g2pool.tile([P, 2, 4 * P, 2], F32, name="grp2_" + label, tag="grp2", align_bytes=64)
+
+        def ev_T1c2(o, engs):
+            b, op = divmod(o, 2)
+            if op == 0:
+                st[("g2", b)] = new_grp2("b%d" % b)
+            g = st[("g2", b)]
+            for half in range(2):
+                tp = st[("t1", o)][half]
+                dst = g[:, op, 2 * P * half:2 * P * (half + 1), :].rearrange("p (a r) u -> p a r u", a=2)
+                src = tp[:].rearrange("p a u r -> p a r u")
+                if engs[half] == "s":
+                    nc.scalar.copy(out=dst, in_=src)
+                else:
+                    nc.vector.tensor_copy(out=dst, in_=src)
+
+        def ev_Q2(b):
+            q = q2pool.tile([P, 2, TB * P], U32, name="qq%d" % b, tag="qq", align_bytes=64)
+            s = q2pool.tile([P, 2, TB * P], U8, name="ss%d" % b, tag="ss", align_bytes=64)
+            nc.vector.quantize_mx(out=q[:].rearrange("p o c -> p (o c)").bitcast(FP8X4),
+                                  scales=s[:].rearrange("p o c -> p (o c)"),
+                                  in_=st[("g2", b)][:].rearrange("p o c u -> p (o c u)").bitcast(BF16))
+            for op in range(2):
+                qs[2 * b + op] = (q[:, op, :], s[:, op, :])
+
+        def ev_AZs2(b, i):
+            nc.scalar.activation(out=zsts[b][:, i:i + 2, :], in_=zsts[b][:, i:i + 2, :], func=ACT.Tanh)
 
         def new_grp(label):
             return gpool.tile([P, 4 * P, 2], F32, name="grp_" + label, tag="grp", align_bytes=64)
@@ -281,6 +319,9 @@ def tile_koslmcell_pa_t_kernel(tc, x, h_prev, c_prev, W_ih, b_ih, W_hh, b_hh,
         def ev_STi(c, i, n):
             nc.sync.dma_start(out=dram(outs[2], c * TB + i, n), in_=ists[c][:, i:i + n, :])
 
+        def ev_STzs(c, i, n):
+            nc.scalar.dma_start(out=dram(outs[0], c * TB + i, n), in_=zsts[c][:, i:i + n, :])
+
         def ev_STz(c, i, n):
             nc.sync.dma_start(out=dram(outs[0], c * TB + i, n), in_=zsts[c][:, i:i + n, :])
 
@@ -310,7 +351,6 @@ def tile_koslmcell_pa_t_kernel(tc, x, h_prev, c_prev, W_ih, b_ih, W_hh, b_hh,
         def WT1(op, half, engs):
             w_T1p(op, half)
             w_T1c(op, half, engs)
-
         ev_T1pp(0, "v")
         ev_T1pp(1, "v")
         ev_T1pt(0)
@@ -331,10 +371,10 @@ def tile_koslmcell_pa_t_kernel(tc, x, h_prev, c_prev, W_ih, b_ih, W_hh, b_hh,
         w_Q(1, 1)
         vec_bits()
         w_T1pt(0, 0)
-        w_T1c(0, 0, "sv")
+        w_T1c(0, 0, "ss")
         w_Q(0, 0)
         w_T1pt(1, 0)
-        w_T1c(1, 0, "sv")
+        w_T1c(1, 0, "ss")
         w_Q(1, 0)
 
         def nv(b):
@@ -345,8 +385,6 @@ def tile_koslmcell_pa_t_kernel(tc, x, h_prev, c_prev, W_ih, b_ih, W_hh, b_hh,
             for h in range(2):
                 if o + h < 2 * NB:
                     T1(o + h, ("ss", "ss")[h] if b == 0 else ("ss", "ss" if b % 2 else "sv")[h])
-                    if b == 0:
-                        load(h, 24, 4, 0)
                 if c >= 0:
                     for i in (2 * h, 2 * h + 1):
                         ev_TBp(c, i)
@@ -355,6 +393,8 @@ def tile_koslmcell_pa_t_kernel(tc, x, h_prev, c_prev, W_ih, b_ih, W_hh, b_hh,
                             ev_TBsv(c, i)
                         else:
                             ev_TBs(c, i)
+                    if 5 <= c < NB - 1:
+                        ev_STm(c, 2 * h, 2)
                     if b == NB:
                         ev_STm(c, 2 * h, 2)
                         if h == 0:
@@ -367,15 +407,21 @@ def tile_koslmcell_pa_t_kernel(tc, x, h_prev, c_prev, W_ih, b_ih, W_hh, b_hh,
                                 if i in (1, 3):
                                     ev_STi(c, i - 1, 2)
             if b == 0:
+                load(0, 24, 8, 0)
+                load(1, 24, 8, 0)
                 load(2, 24, 8, 24)
-                load(0, 28, 4, 4)
-                load(1, 28, 4, 4)
             if b < NB:
                 if c >= 0:
-                    ev_STm(c, 0, TB)
+                    if c < 5:
+                        ev_STm(c, 0, TB)
                     ev_FA(c, 0, 2)
+                    if c >= 5:
+                        ev_STi(c, 0, 2)
                     ev_FA(c, 2, 2)
-                    ev_STi(c, 0, TB)
+                    if c >= 5:
+                        ev_STi(c, 2, 2)
+                    else:
+                        ev_STi(c, 0, TB)
                 for b2 in ((0, 1) if b == 0 else (b + 1,)):
                     if b2 < NB:
                         for i in range(nv(b2)):
@@ -395,4 +441,7 @@ def tile_koslmcell_pa_t_kernel(tc, x, h_prev, c_prev, W_ih, b_ih, W_hh, b_hh,
                     ev_AZp(b, i)
                     ev_AZv(b, i)
                     ev_AZs(b, i)
-                ev_STz(b, 0, TB)
+                    if b >= 6 and i % 2 == 1:
+                        ev_STz(b, i - 1, 2)
+                if b < 6:
+                    ev_STz(b, 0, TB)

@@ -28,7 +28,7 @@ def tile_koslmcell_pa_t_kernel(tc, x, h_prev, c_prev, W_ih, b_ih, W_hh, b_hh,
         const = ctx.enter_context(tc.tile_pool(name="const", bufs=1))
         resid = ctx.enter_context(tc.tile_pool(name="resid", bufs=1))
         gpool = ctx.enter_context(tc.tile_pool(name="gpool", bufs=4))
-        qpool = ctx.enter_context(tc.tile_pool(name="qpool", bufs=1))
+        qpool = ctx.enter_context(tc.tile_pool(name="qpool", bufs=3))
         tpool = ctx.enter_context(tc.tile_pool(name="tpool", bufs=8))
         stage = ctx.enter_context(tc.tile_pool(name="stage", bufs=3))
         g2pool = ctx.enter_context(tc.tile_pool(name="g2pool", bufs=2))

@@ -355,17 +355,15 @@ def tile_koslmcell_pa_t_kernel(tc, x, h_prev, c_prev, W_ih, b_ih, W_hh, b_hh,
         ev_T1pp(1, "v")
         ev_T1pt(0)
         ev_T1c(0, "sv")
-        w_T1pp(0, 1, "v")
         ev_Q(0)
         ev_T1pt(1)
         ev_T1c(1, "sv")
-        w_T1pp(1, 1, "v")
         ev_Q(1)
-        w_T1pt(0, 1)
+        w_T1p(0, 1)
         w_T1c(0, 1, "ss")
         w_T1pp(0, 0, "v")
         w_Q(0, 1)
-        w_T1pt(1, 1)
+        w_T1p(1, 1)
         w_T1c(1, 1, "ss")
         w_T1pp(1, 0, "v")
         w_Q(1, 1)

@@ -351,12 +351,10 @@ def tile_koslmcell_pa_t_kernel(tc, x, h_prev, c_prev, W_ih, b_ih, W_hh, b_hh,
         def WT1(op, half, engs):
             w_T1p(op, half)
             w_T1c(op, half, engs)
-        ev_T1pp(0, "v")
-        ev_T1pp(1, "v")
-        ev_T1pt(0)
+        ev_T1p(0)
         ev_T1c(0, "sv")
         ev_Q(0)
-        ev_T1pt(1)
+        ev_T1p(1)
         ev_T1c(1, "sv")
         ev_Q(1)
         w_T1p(0, 1)
@@ -376,13 +374,13 @@ def tile_koslmcell_pa_t_kernel(tc, x, h_prev, c_prev, W_ih, b_ih, W_hh, b_hh,
         w_Q(1, 0)
 
         def nv(b):
-            return 4 if b == 0 else 1 if b == 1 else (1 if b % 2 else 0)
+            return 4 if b == 0 else 1 if b == 1 else (0 if b % 2 else 0)
         for b in range(NB + 1):
             c = b - 1
             o = 2 * b + 2
             for h in range(2):
                 if o + h < 2 * NB:
-                    T1(o + h, ("ss", "ss")[h] if b == 0 else ("ss", "ss" if b % 2 else "sv")[h])
+                    T1(o + h, ("ss", "ss")[h] if b == 0 else ("ss", "sv" if b % 2 else "sv")[h])
                 if c >= 0:
                     for i in (2 * h, 2 * h + 1):
                         ev_TBp(c, i)

from contextlib import ExitStack

import concourse.mybir as mybir
from concourse.masks import make_identity

F32 = mybir.dt.float32
BF16 = mybir.dt.bfloat16
U32 = mybir.dt.uint32
U8 = mybir.dt.uint8
FP8X4 = mybir.dt.float8_e4m3fn_x4
ACT = mybir.ActivationFunctionType
ALU = mybir.AluOpType

P = 128
B, D, H = 4096, 512, 512
NT = B // P
TG = 8
TB = 4
NB = NT // TB
M_SCALE = 1.5
FLOPS = 2 * B * (2 * H) * (D + H)


def tile_koslmcell_pa_t_kernel(tc, x, h_prev, c_prev, W_ih, b_ih, W_hh, b_hh,
                                          log_lambda, z_bias, m_bias, out_0, out_1, out_2):
    nc = tc.nc
    with ExitStack() as ctx:
        const = ctx.enter_context(tc.tile_pool(name="const", bufs=1))
        resid = ctx.enter_context(tc.tile_pool(name="resid", bufs=1))
        gpool = ctx.enter_context(tc.tile_pool(name="gpool", bufs=4))
        qpool = ctx.enter_context(tc.tile_pool(name="qpool", bufs=3))
        tpool = ctx.enter_context(tc.tile_pool(name="tpool", bufs=8))
        stage = ctx.enter_context(tc.tile_pool(name="stage", bufs=3))
        g2pool = ctx.enter_context(tc.tile_pool(name="g2pool", bufs=2))
        q2pool = ctx.enter_context(tc.tile_pool(name="q2pool", bufs=3))
        mstp = ctx.enter_context(tc.tile_pool(name="mstp", bufs=4))
        ps = ctx.enter_context(tc.psum_pool(name="ps", bufs=8))
        ctx.enter_context(tc.manual_schedule())

        def row(v):
            return v.rearrange("(o n) -> o n", o=1)

        warm = const.tile([P, 2], F32, name="warm")
        nc.vector.memset(warm[:], 0.0)
        nc.scalar.activation(out=warm[:, 1:2], in_=warm[:, 0:1], func=ACT.Tanh)
        vecs = const.tile([P, 3 * H], BF16, name="vecs")
        nc.vector.memset(vecs[:], 0.0)
        ones = const.tile([P, P], BF16, name="ones")
        nc.vector.memset(ones[:], 1.0)
        ident = const.tile([P, P], F32, name="ident")
        make_identity(nc, ident[:])

        views = [v.rearrange("(g p t) k -> g p t k", p=P, t=TG) for v in (x, h_prev, c_prev)]
        outs = [o.rearrange("(g p t) n -> g p t n", p=P, t=TG) for o in (out_0, out_1, out_2)]

        def dram(view, t0, n):
            return view[t0 // TG, :, t0 % TG:t0 % TG + n, :]
        where = [{}, {}, {}]

        def load(i, t0, n, tag):
            rt = resid.tile([P, n * D], BF16, name="in%d_%d" % (i, t0), tag="%s%d" % ("xhc"[i], tag))
            nc.sync.dma_start(out=rt[:].rearrange("p (t k) -> p t k", k=D), in_=dram(views[i], t0, n))
            for j in range(n):
                where[i][t0 + j] = (rt, j)

        def load_half(i, t0, rt, j0, n):
            nc.sync.dma_start(out=rt[:, j0 * D:(j0 + n) * D].rearrange("p (t k) -> p t k", k=D), in_=dram(views[i], t0, n))
            for j in range(n):
                where[i][t0 + j] = (rt, j0 + j)

        def load_w(op, half, tag):
            w = (W_ih, W_hh)[op]
            wr = stage.tile([P, 4 * D], BF16, name="wraw%d%d" % (op, half), tag=tag)
            nc.sync.dma_start(out=wr[:], in_=w[half * H:(half + 1) * H, :].rearrange("(p a) k -> p (a k)", a=4))
            return wr

        first = {}
        for i in range(2):
            first[i] = resid.tile([P, 8 * D], BF16, name="in%d_0" % i, tag="%s0" % "xh"[i])
        load_half(0, 0, first[0], 0, 4)
        load_half(1, 0, first[1], 0, 4)
        wraw = {}
        wraw[(0, 1)] = load_w(0, 1, "zst")
        wraw[(1, 1)] = load_w(1, 1, "ist")
        nc.sync.dma_start(out=vecs[0:1, 0:2 * H], in_=row(b_ih))
        nc.sync.dma_start(out=vecs[1:2, 0:2 * H], in_=row(b_hh))
        nc.sync.dma_start(out=vecs[2:3, 0:H], in_=row(z_bias))
        nc.sync.dma_start(out=vecs[2:3, H:2 * H], in_=row(m_bias))
        nc.sync.dma_start(out=vecs[0:1, 2 * H:3 * H], in_=row(log_lambda))
        wraw[(0, 0)] = load_w(0, 0, "zst")
        wraw[(1, 0)] = load_w(1, 0, "ist")
        load_half(0, 4, first[0], 4, 4)
        load_half(1, 4, first[1], 4, 4)
        load(2, 0, 8, 0)
        load(0, 8, 8, 8)
        load(1, 8, 8, 8)
        load(2, 8, 8, 8)
        load(0, 16, 8, 16)
        load(1, 16, 8, 16)
        load(2, 16, 8, 16)

        wq = const.tile([P, 2, 2 * H], U32, name="wq", align_bytes=64)
        wsc = const.tile([P, 2, 2 * H], U8, name="wsc", align_bytes=64)


        def permuted(words, label, eng):
            pm = gpool.tile([P, 4, 2, P], F32, name="pm_" + label, tag="grp", align_bytes=64)
            src = words.rearrange("p (a w u) -> p a u w", a=4, u=2)
            if eng == "v":
                nc.vector.tensor_copy(out=pm[:], in_=src)
            else:
                nc.scalar.copy(out=pm[:], in_=src)
            return pm

        def t1_pe(srcs, label):
            banks = []
            for half in range(2):
                tp = ps.tile([P, 2, 2, P], F32, name="tp_%s_%d" % (label, half), tag="ps")
                for a in range(2):
                    for u in range(2):
                        if isinstance(srcs, list):
                            nc.tensor.transpose(tp[:, a, u, :], srcs[2 * half + a][:, u:2 * P:2], ident[:])
                        else:
                            nc.tensor.transpose(tp[:, a, u, :], srcs[:, 2 * half + a, u, :], ident[:])
                banks.append(tp)
            return banks

        def t1_copy(banks, grouped, half, eng, inter):
            tp = banks[half]
            if inter:
                dst = grouped[:].rearrange("p (r a) u -> p r a u", a=4)[:, :, 2 * half:2 * half + 2, :]
                src = tp[:].rearrange("p a u r -> p r a u")
            else:
                dst = grouped[:, 2 * P * half:2 * P * (half + 1), :].rearrange("p (a r) u -> p a r u", a=2)
                src = tp[:].rearrange("p a u r -> p a r u")
            if eng == "s":
                nc.scalar.copy(out=dst, in_=src)
            else:
                nc.vector.tensor_copy(out=dst, in_=src)

        def new_grp2(label):
            return g2pool.tile([P, 2, 4 * P, 2], F32, name="grp2_" + label, tag="grp2", align_bytes=64)

        def ev_T1c2(o, engs):
            b, op = divmod(o, 2)
            if op == 0:
                st[("g2", b)] = new_grp2("b%d" % b)
            g = st[("g2", b)]
            for half in range(2):
                tp = st[("t1", o)][half]
                dst = g[:, op, 2 * P * half:2 * P * (half + 1), :].rearrange("p (a r) u -> p a r u", a=2)
                src = tp[:].rearrange("p a u r -> p a r u")
                if engs[half] == "s":
                    nc.scalar.copy(out=dst, in_=src)
                else:
                    nc.vector.tensor_copy(out=dst, in_=src)

        def ev_Q2(b):
            q = q2pool.tile([P, 2, TB * P], U32, name="qq%d" % b, tag="qq", align_bytes=64)
            s = q2pool.tile([P, 2, TB * P], U8, name="ss%d" % b, tag="ss", align_bytes=64)
            nc.vector.quantize_mx(out=q[:].rearrange("p o c -> p (o c)").bitcast(FP8X4),
                                  scales=s[:].rearrange("p o c -> p (o c)"),
                                  in_=st[("g2", b)][:].rearrange("p o c u -> p (o c u)").bitcast(BF16))
            for op in range(2):
                qs[2 * b + op] = (q[:, op, :], s[:, op, :])

        def ev_AZs2(b, i):
            nc.scalar.activation(out=zsts[b][:, i:i + 2, :], in_=zsts[b][:, i:i + 2, :], func=ACT.Tanh)

        def new_grp(label):
            return gpool.tile([P, 4 * P, 2], F32, name="grp_" + label, tag="grp", align_bytes=64)

        def quantise(grouped, codes, scales):
            nc.vector.quantize_mx(out=codes.bitcast(FP8X4), scales=scales,
                                  in_=grouped[:].rearrange("p c u -> p (c u)").bitcast(BF16))

        st = {}
        qs = {}

        def w_srcs(op, half):
            wv = wraw[(op, half)][:].bitcast(F32)
            return [wv[:, a * (D // 2):(a + 1) * (D // 2)] for a in range(4)]

        def in_srcs(o):
            b, op = divmod(o, 2)
            srcs = []
            for t in range(b * TB, (b + 1) * TB):
                rt, j = where[op][t]
                srcs.append(rt[:].bitcast(F32)[:, j * (D // 2):(j + 1) * (D // 2)])
            return srcs

        def ev_T1pp(o, eng):
            b, op = divmod(o, 2)
            rt, j = where[op][b * TB]
            st[("pm", o)] = permuted(rt[:].bitcast(F32)[:, j * (D // 2):(j + 4) * (D // 2)], "i%d" % o, eng)

        def ev_T1pt(o):
            st[("t1", o)] = t1_pe(st[("pm", o)], "i%d" % o)

        def w_T1pp(op, half, eng):
            st[("wpm", op, half)] = permuted(wraw[(op, half)][:].bitcast(F32), "w%d%d" % (op, half), eng)

        def w_T1pt(op, half):
            st[("wt1", op, half)] = t1_pe(st[("wpm", op, half)], "w%d%d" % (op, half))

        def ev_T1p(o):
            st[("t1", o)] = t1_pe(in_srcs(o), "i%d" % o)

        def ev_T1c(o, engs):
            g = new_grp("i%d" % o)
            st[("g", o)] = g
            for half in range(2):
                t1_copy(st[("t1", o)], g, half, engs[half], False)

        def ev_Q(o):
            b, op = divmod(o, 2)
            q = qpool.tile([P, TB * P], U32, name="q%d" % o, tag="q%d" % op, align_bytes=64)
            s = qpool.tile([P, TB * P], U8, name="s%d" % o, tag="s%d" % op, align_bytes=64)
            quantise(st[("g", o)], q[:], s[:])
            qs[o] = (q, s)

        def w_T1p(op, half):
            st[("wt1", op, half)] = t1_pe(w_srcs(op, half), "w%d%d" % (op, half))

        def w_T1c(op, half, engs):
            g = new_grp("w%d%d" % (op, half))
            st[("wg", op, half)] = g
            for h2 in range(2):
                t1_copy(st[("wt1", op, half)], g, h2, engs[h2], True)

        def w_Q(op, half):
            quantise(st[("wg", op, half)], wq[:, op, half * H:(half + 1) * H], wsc[:, op, half * H:(half + 1) * H])

        msts, zsts, ists = {}, {}, {}

        def ev_CS(b, i):
            if i == 0:
                msts[b] = mstp.tile([P, TB, H], F32, name="mst%d" % b, tag="mst")
            ct, j = where[2][b * TB + i]
            nc.gpsimd.tensor_tensor(out=msts[b][:, i, :], in0=ct[:, j * H:(j + 1) * H], in1=lam15[:], op=ALU.mult)

        def ev_AMp(b, j):
            am = ps.tile([P, TB * P], F32, name="am%d_%d" % (b, j), tag="ps")
            for op in range(2):
                q, s = qs[2 * b + op]
                nc.tensor.matmul_mx(out=am[:], lhsT=wq[:, op, H + j * P:H + (j + 1) * P].bitcast(FP8X4),
                                    lhsT_scale=wsc[:, op, H + j * P:H + (j + 1) * P],
                                    rhs=q[:].bitcast(FP8X4), rhs_scale=s[:], start=(op == 0), stop=(op == 1))
            st[("am", b, j)] = am

        def ev_AMs(b, j):
            tm = tpool.tile([P, TB * P], F32, name="tm%d_%d" % (b, j), tag="tm")
            nc.scalar.activation(out=tm[:], in_=st[("am", b, j)][:], func=ACT.Tanh, bias=bias_m[:, j:j + 1])
            st[("tm", b, j)] = tm

        def ev_AZp(b, i):
            if i == 0:
                zsts[b] = stage.tile([P, TB, H], F32, name="zst%d" % b, tag="zst")
            cols = slice(i * P, (i + 1) * P)
            az = ps.tile([P, H], F32, name="az%d_%d" % (b, i), tag="ps")
            for op in range(2):
                q, s = qs[2 * b + op]
                nc.tensor.matmul_mx(out=az[:], lhsT=q[:, cols].bitcast(FP8X4), lhsT_scale=s[:, cols],
                                    rhs=wq[:, op, 0:H].bitcast(FP8X4), rhs_scale=wsc[:, op, 0:H],
                                    start=(op == 0), stop=(op == 1))
            st[("az", b, i)] = az

        def ev_AZv(b, i):
            nc.vector.tensor_tensor(out=zsts[b][:, i, :], in0=st[("az", b, i)][:], in1=bias_z[:], op=ALU.add)

        def ev_AZs(b, i):
            nc.scalar.activation(out=zsts[b][:, i, :], in_=zsts[b][:, i, :], func=ACT.Tanh)

        def ev_TBp(c, i):
            if i == 0:
                ists[c] = stage.tile([P, TB, H], F32, name="ist%d" % c, tag="ist")
            cols = slice(i * P, (i + 1) * P)
            tb = ps.tile([P, H], F32, name="tb%d_%d" % (c, i), tag="ps")
            for j in range(4):
                nc.tensor.transpose(tb[:, j * P:(j + 1) * P], st[("tm", c, j)][:, cols], ident[:])
            st[("tb", c, i)] = tb

        def ev_TBv(c, i):
            nc.vector.tensor_tensor(out=ists[c][:, i, :], in0=st[("tb", c, i)][:], in1=msts[c][:, i, :], op=ALU.mult)

        def ev_TBs(c, i):
            nc.scalar.mul(out=msts[c][:, i, :], in_=st[("tb", c, i)][:], mul=M_SCALE)

        def ev_TBsv(c, i):
            nc.vector.tensor_scalar(out=msts[c][:, i, :], in0=st[("tb", c, i)][:], scalar1=M_SCALE, scalar2=0.0, op0=ALU.mult, op1=ALU.add)

        def ev_FA(c, i, n):
            nc.vector.tensor_tensor(out=ists[c][:, i:i + n, :], in0=ists[c][:, i:i + n, :], in1=zsts[c][:, i:i + n, :], op=ALU.add)

        def ev_FAg(c, i):
            nc.gpsimd.tensor_tensor(out=ists[c][:, i, :], in0=ists[c][:, i, :], in1=zsts[c][:, i, :], op=ALU.add)

        def ev_trig():
            nc.vector.tensor_copy(out=lamg[:, 0:1], in_=lam15[:, 0:1])

        def ev_CS1(b, i, eng):
            if b not in msts:
                msts[b] = mstp.tile([P, TB, H], F32, name="mst%d" % b, tag="mst")
            ct, j = where[2][b * TB + i]
            if eng == "g":
                nc.gpsimd.tensor_tensor(out=msts[b][:, i, :], in0=ct[:, j * H:(j + 1) * H], in1=lamg[:], op=ALU.mult)
            else:
                nc.vector.tensor_tensor(out=msts[b][:, i, :], in0=ct[:, j * H:(j + 1) * H], in1=lam15[:], op=ALU.mult)

        def ev_CSv(b, i):
            if i == 0:
                msts[b] = mstp.tile([P, TB, H], F32, name="mst%d" % b, tag="mst")
            ct, j = where[2][b * TB + i]
            nc.vector.tensor_tensor(out=msts[b][:, i, :], in0=ct[:, j * H:(j + 1) * H], in1=lam15[:], op=ALU.mult)

        def ev_STm(c, i, n):
            nc.sync.dma_start(out=dram(outs[1], c * TB + i, n), in_=msts[c][:, i:i + n, :])

        def ev_STi(c, i, n):
            nc.sync.dma_start(out=dram(outs[2], c * TB + i, n), in_=ists[c][:, i:i + n, :])

        def ev_STzs(c, i, n):
            nc.scalar.dma_start(out=dram(outs[0], c * TB + i, n), in_=zsts[c][:, i:i + n, :])

        def ev_STz(c, i, n):
            nc.sync.dma_start(out=dram(outs[0], c * TB + i, n), in_=zsts[c][:, i:i + n, :])


        bias_z = const.tile([P, H], F32, name="bias_z")
        lam = const.tile([P, H], F32, name="lam")
        lam15 = const.tile([P, H], F32, name="lam15")
        lamg = const.tile([P, H], F32, name="lamg")
        bias_m = const.tile([P, 4], F32, name="bias_m")
        def vec_bits():
            bzp = ps.tile([P, H], F32, name="bzp", tag="ps")
            nc.tensor.matmul(out=bzp[:], lhsT=ones[:], rhs=vecs[:, 0:H], start=True, stop=True)
            nc.vector.tensor_copy(out=bias_z[:], in_=bzp[:])
            lmp = ps.tile([P, H], F32, name="lmp", tag="ps")
            nc.tensor.matmul(out=lmp[:], lhsT=ones[:], rhs=vecs[:, 2 * H:3 * H], start=True, stop=True)
            nc.scalar.activation(out=lam[:], in_=lmp[:], func=ACT.Exp)
            nc.gpsimd.tensor_scalar(out=lam15[:], in0=lam[:], scalar1=M_SCALE, scalar2=0.0, op0=ALU.mult, op1=ALU.add)
            nc.gpsimd.tensor_scalar(out=lamg[:], in0=lam[:], scalar1=M_SCALE, scalar2=0.0, op0=ALU.mult, op1=ALU.add)
            pp = ps.tile([P, 4, 32], F32, name="pp", tag="ps")
            for j in range(4):
                nc.tensor.matmul(out=pp[:, j, :], lhsT=vecs[:, H + j * P:H + (j + 1) * P], rhs=ones[:, 0:32],
                                 start=True, stop=True)
            nc.scalar.copy(out=bias_m[:], in_=pp[:, :, 0])
        def T1(o, engs):
            ev_T1p(o)
            ev_T1c(o, engs)
        def WT1(op, half, engs):
            w_T1p(op, half)
            w_T1c(op, half, engs)
        ev_T1p(0)
        ev_T1c(0, "sv")
        ev_Q(0)
        ev_T1p(1)
        ev_T1c(1, "sv")
        ev_Q(1)
        w_T1p(0, 1)
        w_T1c(0, 1, "ss")
        w_T1pp(0, 0, "v")
        w_Q(0, 1)
        w_T1p(1, 1)
        w_T1c(1, 1, "ss")
        w_T1pp(1, 0, "v")
        w_Q(1, 1)
        vec_bits()
        w_T1pt(0, 0)
        w_T1c(0, 0, "ss")
        w_Q(0, 0)
        w_T1pt(1, 0)
        w_T1c(1, 0, "ss")
        w_Q(1, 0)

        def nv(b):
            return 4 if b == 0 else 1 if b == 1 else (0 if b % 2 else 0)
        for b in range(NB + 1):
            c = b - 1
            o = 2 * b + 2
            for h in range(2):
                if o + h < 2 * NB:
                    T1(o + h, ("ss", "ss")[h] if b == 0 else ("ss", "sv" if b % 2 else "sv")[h])
                if c >= 0:
                    for i in (2 * h, 2 * h + 1):
                        ev_TBp(c, i)
                        ev_TBv(c, i)
                        if b == NB and i in ():
                            ev_TBsv(c, i)
                        else:
                            ev_TBs(c, i)
                    if 5 <= c < NB - 1:
                        ev_STm(c, 2 * h, 2)
                    if b == NB:
                        ev_STm(c, 2 * h, 2)
                        if h == 0:
                            for i in (0,):
                                ev_FAg(c, i)
                        else:
                            for i in range(4):
                                if i not in (0,):
                                    ev_FA(c, i, 1)
                                if i in (1, 3):
                                    ev_STi(c, i - 1, 2)
            if b == 0:
                load(0, 24, 8, 0)
                load(1, 24, 8, 0)
                load(2, 24, 8, 24)
            if b < NB:
                if c >= 0:
                    if c < 5:
                        ev_STm(c, 0, TB)
                    ev_FA(c, 0, 2)
                    if c >= 5:
                        ev_STi(c, 0, 2)
                    ev_FA(c, 2, 2)
                    if c >= 5:
                        ev_STi(c, 2, 2)
                    else:
                        ev_STi(c, 0, TB)
                for b2 in ((0, 1) if b == 0 else (b + 1,)):
                    if b2 < NB:
                        for i in range(nv(b2)):
                            ev_CS1(b2, i, "v")
                for h in range(2):
                    if o + h < 2 * NB:
                        ev_Q(o + h)
                ev_trig()
                for b2 in ((0, 1) if b == 0 else (b + 1,)):
                    if b2 < NB:
                        for i in range(nv(b2), 4):
                            ev_CS1(b2, i, "g")
                for j in range(4):
                    ev_AMp(b, j)
                    ev_AMs(b, j)
                for i in range(4):
                    ev_AZp(b, i)
                    ev_AZv(b, i)
                    ev_AZs(b, i)
                    if b >= 6 and i % 2 == 1:
                        ev_STz(b, i - 1, 2)
                if b < 6:
                    ev_STz(b, 0, TB)
